import numpy as np
import ml_dtypes


def mxq(x, axis, fmt="e4m3"):
    dtype, down = {"e4m3": (ml_dtypes.float8_e4m3fn, 7), "e5m2": (ml_dtypes.float8_e5m2, 14)}[fmt]
    v = np.moveaxis(np.asarray(x, np.float32).astype(ml_dtypes.bfloat16).astype(np.float64), axis, -1)
    blocks = v.reshape(v.shape[:-1] + (-1, 32))
    amax = np.abs(blocks).max(-1, keepdims=True)
    byte = np.maximum(np.where(amax > 0, np.frexp(amax)[1] - 1 + 127, 0) - down, 1)
    scale = np.exp2(byte - 127.0)
    codes = (blocks / scale).astype(np.float32).astype(dtype).astype(np.float64)
    return np.moveaxis((codes * scale).reshape(v.shape), -1, axis)


WIDE = False


def mx_kscale(k):
    if not WIDE:
        return np.ones(k)
    levels = np.array([10, -10, 5, -5, 0])
    a = np.random.permutation(np.resize(levels, k // 512 * 4)).reshape(k // 512, 4)
    idx = np.arange(k)
    return np.exp2(a[idx // 512, idx % 128 // 32])


BF16 = ml_dtypes.bfloat16


def bf(x):
    return np.asarray(x, np.float32).astype(BF16)


def f64(x):
    return np.asarray(x).astype(np.float64)


B, N, E, H, G, C, EO = 1, 2048, 1024, 8, 128, 512, 1024
D = E // H
NB = N // C


def silu(v):
    return v / (1.0 + np.exp(-v))


def setup_inputs():
    s = mx_kscale(N)
    return {"q": bf(silu(0.4 * np.random.standard_normal((B, H, N, D)))),
            "k": bf(silu(0.4 * np.random.standard_normal((B, H, N, D))) * s[:, None]),
            "v": bf(silu(0.4 * np.random.standard_normal((B, H, N, D))) / s[:, None]),
            "log_slope": bf(-(3.0 + 5.0 * np.random.random(H)) / N)}


def reference(q, k, v, log_slope):
    ls = f64(log_slope)
    vq = mxq(f64(v), 2, "e4m3")
    idx = np.arange(N, dtype=np.float64)
    outs = []
    for i in range(NB):
        lo, hi = i * C, (i + 1) * C
        diff = idx[lo:hi, None] - idx[None, :hi]
        decay = np.where(diff >= 0, np.exp(ls[:, None, None] * np.maximum(diff, 0.0)), 0.0)
        energy = (f64(q)[:, :, lo:hi] @ f64(k)[:, :, :hi].transpose(0, 1, 3, 2)) * decay
        outs.append(mxq(energy, 3, "e4m3") @ vq[:, :, :hi])
    return np.concatenate(outs, axis=2)

@@ -1,0 +1,220 @@
+from contextlib import ExitStack
+
+import concourse.mybir as mybir
+from concourse.masks import make_identity
+
+F32 = mybir.dt.float32
+BF16 = mybir.dt.bfloat16
+I32 = mybir.dt.int32
+U32 = mybir.dt.uint32
+U8 = mybir.dt.uint8
+FP8X4 = mybir.dt.float8_e4m3fn_x4
+ALU = mybir.AluOpType
+ACT = mybir.ActivationFunctionType
+
+P = 128
+PACK = 4
+K_PASS = P * PACK
+HEADS = 8
+SEQ = 2048
+HEAD_DIM = 128
+BLOCK = 512
+N_TILES = SEQ // P
+N_BLOCKS = SEQ // BLOCK
+TILES_PER_BLOCK = BLOCK // P
+FAR_STEPS = N_TILES - PACK
+
+FLOPS = 2 * 2 * HEADS * HEAD_DIM * BLOCK * BLOCK * (N_BLOCKS * (N_BLOCKS + 1) // 2)
+
+
+def tile_tnlattention_pa_kernel(tc, q, k, v, log_slope, out):
+    nc = tc.nc
+    with ExitStack() as ctx:
+        const = ctx.enter_context(tc.tile_pool(name="const", bufs=1))
+        rows = ctx.enter_context(tc.tile_pool(name="rows", bufs=2))
+        head = ctx.enter_context(tc.tile_pool(name="head", bufs=2))
+        work = ctx.enter_context(tc.tile_pool(name="work", bufs=2))
+        psum_s = ctx.enter_context(tc.psum_pool(name="psum_s", bufs=4))
+        psum_o = ctx.enter_context(tc.psum_pool(name="psum_o", bufs=2))
+        psum_t = ctx.enter_context(tc.psum_pool(name="psum_t", bufs=2))
+        ctx.enter_context(tc.manual_schedule())
+
+        slope_bf = const.tile([P, HEADS], BF16)
+        nc.sync.dma_start(out=slope_bf[:], in_=log_slope.partition_broadcast(P))
+
+        ident = const.tile([P, P], BF16)
+        make_identity(nc, ident[:])
+
+        dist_int = const.tile([P, P, PACK], I32)
+        nc.gpsimd.iota(dist_int[:], pattern=[[1, P], [-P, PACK]], base=(PACK - 1) * P, channel_multiplier=-1)
+        step_int = const.tile([P, FAR_STEPS], I32)
+        nc.gpsimd.iota(step_int[:], pattern=[[P, FAR_STEPS]], base=0, channel_multiplier=0)
+
+        dist = const.tile([P, P, PACK], F32)
+        nc.vector.tensor_copy(out=dist[:], in_=dist_int[:])
+        dist_clamped = const.tile([P, P, PACK], F32)
+        nc.vector.tensor_scalar_max(out=dist_clamped[:], in0=dist[:], scalar1=0.0)
+        causal = const.tile([P, P, PACK], F32)
+        nc.vector.tensor_single_scalar(out=causal[:], in_=dist[:], scalar=0.0, op=ALU.is_ge)
+        step = const.tile([P, FAR_STEPS], F32)
+        nc.vector.tensor_copy(out=step[:], in_=step_int[:])
+
+        slope = const.tile([P, HEADS], F32)
+        nc.vector.tensor_copy(out=slope[:], in_=slope_bf[:])
+        slope_tile = const.tile([P, HEADS], F32)
+        nc.vector.tensor_scalar_mul(out=slope_tile[:], in0=slope[:], scalar1=float(P))
+
+        diag_a = const.tile([P, TILES_PER_BLOCK, P, PACK], BF16, align_bytes=64)
+        diag_b = const.tile([P, TILES_PER_BLOCK, P, PACK], BF16, align_bytes=64)
+        nc.vector.memset(diag_a[:], 0.0)
+        nc.vector.memset(diag_b[:], 0.0)
+        diag_tiles = [diag_a, diag_b]
+
+        loaded = {}
+        ready = {}
+        grouped_of = {}
+        codes_of = {}
+
+        def load(h):
+            k_rows = rows.tile([P, N_TILES, HEAD_DIM], BF16)
+            q_rows = rows.tile([P, N_TILES, HEAD_DIM], BF16)
+            v_rows = rows.tile([P, N_TILES, HEAD_DIM], BF16)
+            nc.sync.dma_start(out=k_rows[:], in_=k[0, h].rearrange("(n p) d -> p n d", p=P))
+            nc.sync.dma_start(out=q_rows[:], in_=q[0, h].rearrange("(n p) d -> p n d", p=P))
+            nc.sync.dma_start(out=v_rows[:], in_=v[0, h].rearrange("(n p) d -> p n d", p=P))
+            loaded[h] = (k_rows, q_rows, v_rows)
+
+        def flip(src_rows, dst_cols):
+            for n0 in range(0, N_TILES, PACK):
+                flipped = psum_t.tile([P, PACK, P], BF16)
+                for j in range(PACK):
+                    nc.tensor.transpose(flipped[:, j, :], src_rows[:, n0 + j, :], ident[:])
+                nc.scalar.copy(
+                    out=dst_cols[:, n0 * P : (n0 + PACK) * P],
+                    in_=flipped[:].rearrange("d j n -> d (j n)"),
+                )
+
+        def prepare(h):
+            k_rows, q_rows, v_rows = loaded[h]
+            slope_h = slope[:, h : h + 1]
+
+            v_grouped = head.tile([P, N_BLOCKS, HEAD_DIM, PACK], BF16, align_bytes=64)
+            nc.scalar.copy(out=v_grouped[:], in_=v_rows[:].rearrange("p (g t) d -> p g d t", t=PACK))
+
+            far = head.tile([P, P, PACK], F32)
+            nc.scalar.activation(out=far[:], in_=dist[:], func=ACT.Exp, bias=slope_tile[:, h : h + 1], scale=slope_h)
+            near_raw = head.tile([P, P, PACK], F32)
+            nc.scalar.activation(out=near_raw[:], in_=dist_clamped[:], func=ACT.Exp, scale=slope_h)
+            near = head.tile([P, P, PACK], F32)
+            nc.gpsimd.tensor_tensor(out=near[:], in0=near_raw[:], in1=causal[:], op=ALU.mult)
+            far_step = head.tile([P, FAR_STEPS], F32)
+            nc.scalar.activation(out=far_step[:], in_=step[:], func=ACT.Exp, scale=slope_h)
+
+            kT = head.tile([P, SEQ], BF16)
+            qT = head.tile([P, SEQ], BF16)
+            flip(k_rows, kT)
+            flip(q_rows, qT)
+
+            v_codes = head.tile([P, N_BLOCKS * HEAD_DIM], U32, align_bytes=64)
+            v_scales = head.tile([P, N_BLOCKS * HEAD_DIM], U8, align_bytes=64)
+            nc.vector.quantize_mx(
+                out=v_codes[:].bitcast(FP8X4),
+                scales=v_scales[:],
+                in_=v_grouped[:].rearrange("p g d t -> p (g d t)"),
+            )
+            ready[h] = (kT, qT, v_codes, v_scales, near, far, far_step)
+
+        def energies(n, h, b, g, r):
+            kT, qT, v_codes, v_scales, near, far, far_step = ready[h]
+            diagonal = g == b
+            live = r + 1 if diagonal else PACK
+            q_tile = b * TILES_PER_BLOCK + r
+            s_bank = psum_s.tile([P, PACK, P], F32)
+            for t in range(live):
+                k_tile = g * PACK + t
+                nc.tensor.matmul(
+                    s_bank[:, t, :],
+                    lhsT=kT[:, k_tile * P : (k_tile + 1) * P],
+                    rhs=qT[:, q_tile * P : (q_tile + 1) * P],
+                    start=True,
+                    stop=True,
+                )
+            s_view = s_bank[:, 0:live, :].rearrange("p t c -> p c t")
+            grouped = grouped_of[n]
+            if diagonal:
+                nc.vector.tensor_tensor(
+                    out=grouped[:, r, :, 0:live], in0=s_view, in1=near[:, :, PACK - live : PACK], op=ALU.mult
+                )
+            else:
+                s = (b - g - 1) * TILES_PER_BLOCK + r
+                nc.vector.scalar_tensor_tensor(
+                    out=grouped[:, r, :, :],
+                    in0=s_view,
+                    scalar=far_step[:, s : s + 1],
+                    in1=far[:],
+                    op0=ALU.mult,
+                    op1=ALU.mult,
+                )
+
+        def quantise(n, h, b, g):
+            e_codes, e_scales = codes_of[(h, b)]
+            nc.vector.quantize_mx(
+                out=e_codes[:, g, :].bitcast(FP8X4),
+                scales=e_scales[:, g, :],
+                in_=grouped_of[n][:].rearrange("p r c t -> p (r c t)"),
+            )
+
+        def second_matmul(h, b):
+            kT, qT, v_codes, v_scales, near, far, far_step = ready[h]
+            e_codes, e_scales = codes_of[(h, b)]
+            o_bank = psum_o.tile([P, TILES_PER_BLOCK, HEAD_DIM], F32)
+            for r in range(TILES_PER_BLOCK):
+                q_cols = slice(r * P, (r + 1) * P)
+                for g in range(b + 1):
+                    v_cols = slice(g * HEAD_DIM, (g + 1) * HEAD_DIM)
+                    nc.tensor.matmul_mx(
+                        out=o_bank[:, r, :],
+                        lhsT=e_codes[:, g, q_cols].bitcast(FP8X4),
+                        lhsT_scale=e_scales[:, g, q_cols],
+                        rhs=v_codes[:, v_cols].bitcast(FP8X4),
+                        rhs_scale=v_scales[:, v_cols],
+                        start=(g == 0),
+                        stop=(g == b),
+                    )
+            o_rows = work.tile([P, TILES_PER_BLOCK, HEAD_DIM], F32)
+            nc.scalar.copy(out=o_rows[:], in_=o_bank[:])
+            nc.sync.dma_start(
+                out=out[0, h, b * BLOCK : (b + 1) * BLOCK, :].rearrange("(r p) d -> p r d", p=P),
+                in_=o_rows[:],
+            )
+
+        units = [(h, b, g) for h in range(HEADS) for b in range(N_BLOCKS) for g in range(b + 1)]
+
+        load(0)
+        prepare(0)
+        load(1)
+        for n, (h, b, g) in enumerate(units):
+            if g == 0:
+                e_codes = work.tile([P, N_BLOCKS, BLOCK], U32, align_bytes=64)
+                e_scales = work.tile([P, N_BLOCKS, BLOCK], U8, align_bytes=64)
+                codes_of[(h, b)] = (e_codes, e_scales)
+                if b == N_BLOCKS - 1 and h + 1 < HEADS:
+                    prepare(h + 1)
+                    if h + 2 < HEADS:
+                        load(h + 2)
+            if g == b:
+                grouped_of[n] = diag_tiles[(h * N_BLOCKS + b) % 2]
+            else:
+                grouped = work.tile([P, TILES_PER_BLOCK, P, PACK], BF16, align_bytes=64)
+                grouped_of[n] = grouped
+            for r in range(TILES_PER_BLOCK):
+                energies(n, h, b, g, r)
+                if r == 0 and n > 0:
+                    quantise(n - 1, *units[n - 1])
+            if n > 0:
+                h_done, b_done, g_done = units[n - 1]
+                if g_done == b_done:
+                    second_matmul(h_done, b_done)
+        last = len(units) - 1
+        quantise(last, *units[last])
+        second_matmul(HEADS - 1, N_BLOCKS - 1)

@@ -14,7 +14,6 @@ ACT = mybir.ActivationFunctionType
 
 P = 128
 PACK = 4
-K_PASS = P * PACK
 HEADS = 8
 SEQ = 2048
 HEAD_DIM = 128
@@ -22,9 +21,15 @@ BLOCK = 512
 N_TILES = SEQ // P
 N_BLOCKS = SEQ // BLOCK
 TILES_PER_BLOCK = BLOCK // P
+UNITS_PER_HEAD = N_BLOCKS * (N_BLOCKS + 1) // 2
 FAR_STEPS = N_TILES - PACK
+FLIP_GROUPS = 2 * N_TILES // PACK
 
-FLOPS = 2 * 2 * HEADS * HEAD_DIM * BLOCK * BLOCK * (N_BLOCKS * (N_BLOCKS + 1) // 2)
+FLOPS = 2 * 2 * HEADS * HEAD_DIM * BLOCK * BLOCK * UNITS_PER_HEAD
+
+
+DIRECT = TILES_PER_BLOCK - 1
+HELPED = TILES_PER_BLOCK - 1
 
 
 def tile_tnlattention_pa_kernel(tc, q, k, v, log_slope, out):
@@ -34,8 +39,8 @@ def tile_tnlattention_pa_kernel(tc, q, k, v, log_slope, out):
         rows = ctx.enter_context(tc.tile_pool(name="rows", bufs=2))
         head = ctx.enter_context(tc.tile_pool(name="head", bufs=2))
         work = ctx.enter_context(tc.tile_pool(name="work", bufs=2))
-        psum_s = ctx.enter_context(tc.psum_pool(name="psum_s", bufs=4))
-        psum_o = ctx.enter_context(tc.psum_pool(name="psum_o", bufs=2))
+        psum_s = ctx.enter_context(tc.psum_pool(name="psum_s", bufs=5))
+        psum_o = ctx.enter_context(tc.psum_pool(name="psum_o", bufs=1))
         psum_t = ctx.enter_context(tc.psum_pool(name="psum_t", bufs=2))
         ctx.enter_context(tc.manual_schedule())
 
@@ -64,108 +69,168 @@ def tile_tnlattention_pa_kernel(tc, q, k, v, log_slope, out):
         slope_tile = const.tile([P, HEADS], F32)
         nc.vector.tensor_scalar_mul(out=slope_tile[:], in0=slope[:], scalar1=float(P))
 
-        diag_a = const.tile([P, TILES_PER_BLOCK, P, PACK], BF16, align_bytes=64)
-        diag_b = const.tile([P, TILES_PER_BLOCK, P, PACK], BF16, align_bytes=64)
+        diag_a = const.tile([P, DIRECT, P, PACK], BF16, align_bytes=64)
+        diag_b = const.tile([P, DIRECT, P, PACK], BF16, align_bytes=64)
         nc.vector.memset(diag_a[:], 0.0)
         nc.vector.memset(diag_b[:], 0.0)
         diag_tiles = [diag_a, diag_b]
 
-        loaded = {}
-        ready = {}
-        grouped_of = {}
+        rows_of = {}
+        cols_of = {}
+        raw_of = {}
+        decay_of = {}
+        v_grouped_of = {}
+        v_of = {}
+        bank_of = {}
+        lifted_of = {}
+        direct_of = {}
+        helped_of = {}
         codes_of = {}
 
         def load(h):
-            k_rows = rows.tile([P, N_TILES, HEAD_DIM], BF16)
-            q_rows = rows.tile([P, N_TILES, HEAD_DIM], BF16)
+            kq_rows = rows.tile([P, 2, N_TILES, HEAD_DIM], BF16)
             v_rows = rows.tile([P, N_TILES, HEAD_DIM], BF16)
-            nc.sync.dma_start(out=k_rows[:], in_=k[0, h].rearrange("(n p) d -> p n d", p=P))
-            nc.sync.dma_start(out=q_rows[:], in_=q[0, h].rearrange("(n p) d -> p n d", p=P))
+            nc.sync.dma_start(out=kq_rows[:, 0], in_=k[0, h].rearrange("(n p) d -> p n d", p=P))
+            nc.sync.dma_start(out=kq_rows[:, 1], in_=q[0, h].rearrange("(n p) d -> p n d", p=P))
             nc.sync.dma_start(out=v_rows[:], in_=v[0, h].rearrange("(n p) d -> p n d", p=P))
-            loaded[h] = (k_rows, q_rows, v_rows)
+            rows_of[h] = (kq_rows, v_rows)
 
-        def flip(src_rows, dst_cols):
-            for n0 in range(0, N_TILES, PACK):
+        def prepare_step(h, u):
+            kq_rows, v_rows = rows_of[h]
+            slope_h = slope[:, h : h + 1]
+            if u == 0:
+                kq_cols = head.tile([P, 2 * SEQ], BF16)
+                cols_of[h] = kq_cols
+                far = head.tile([P, P, PACK], F32)
+                nc.scalar.activation(
+                    out=far[:], in_=dist[:], func=ACT.Exp, bias=slope_tile[:, h : h + 1], scale=slope_h
+                )
+                near_raw = head.tile([P, P, PACK], F32)
+                nc.scalar.activation(out=near_raw[:], in_=dist_clamped[:], func=ACT.Exp, scale=slope_h)
+                far_step = head.tile([P, FAR_STEPS], F32)
+                nc.scalar.activation(out=far_step[:], in_=step[:], func=ACT.Exp, scale=slope_h)
+                raw_of[h] = (near_raw, far, far_step)
+            if u == 1:
+                near_raw, far, far_step = raw_of[h]
+                near = head.tile([P, P, PACK], F32)
+                nc.vector.tensor_tensor(out=near[:], in0=near_raw[:], in1=causal[:], op=ALU.mult)
+                decay_of[h] = (near, far, far_step)
+            if u < FLIP_GROUPS:
+                tiles = kq_rows[:].rearrange("p a n d -> p (a n) d")
                 flipped = psum_t.tile([P, PACK, P], BF16)
                 for j in range(PACK):
-                    nc.tensor.transpose(flipped[:, j, :], src_rows[:, n0 + j, :], ident[:])
+                    nc.tensor.transpose(flipped[:, j, :], tiles[:, u * PACK + j, :], ident[:])
                 nc.scalar.copy(
-                    out=dst_cols[:, n0 * P : (n0 + PACK) * P],
+                    out=cols_of[h][:, u * BLOCK : (u + 1) * BLOCK],
                     in_=flipped[:].rearrange("d j n -> d (j n)"),
                 )
+            if u == 0:
+                v_grouped = head.tile([P, N_BLOCKS, HEAD_DIM, PACK], BF16, align_bytes=64)
+                v_grouped_of[h] = v_grouped
+            if u >= FLIP_GROUPS - N_BLOCKS:
+                g = u - (FLIP_GROUPS - N_BLOCKS)
+                nc.scalar.copy(
+                    out=v_grouped_of[h][:, g],
+                    in_=v_rows[:, g * PACK : (g + 1) * PACK, :].rearrange("p t d -> p d t"),
+                )
 
-        def prepare(h):
-            k_rows, q_rows, v_rows = loaded[h]
-            slope_h = slope[:, h : h + 1]
-
-            v_grouped = head.tile([P, N_BLOCKS, HEAD_DIM, PACK], BF16, align_bytes=64)
-            nc.scalar.copy(out=v_grouped[:], in_=v_rows[:].rearrange("p (g t) d -> p g d t", t=PACK))
-
-            far = head.tile([P, P, PACK], F32)
-            nc.scalar.activation(out=far[:], in_=dist[:], func=ACT.Exp, bias=slope_tile[:, h : h + 1], scale=slope_h)
-            near_raw = head.tile([P, P, PACK], F32)
-            nc.scalar.activation(out=near_raw[:], in_=dist_clamped[:], func=ACT.Exp, scale=slope_h)
-            near = head.tile([P, P, PACK], F32)
-            nc.gpsimd.tensor_tensor(out=near[:], in0=near_raw[:], in1=causal[:], op=ALU.mult)
-            far_step = head.tile([P, FAR_STEPS], F32)
-            nc.scalar.activation(out=far_step[:], in_=step[:], func=ACT.Exp, scale=slope_h)
-
-            kT = head.tile([P, SEQ], BF16)
-            qT = head.tile([P, SEQ], BF16)
-            flip(k_rows, kT)
-            flip(q_rows, qT)
-
+        def quantise_v(h):
             v_codes = head.tile([P, N_BLOCKS * HEAD_DIM], U32, align_bytes=64)
             v_scales = head.tile([P, N_BLOCKS * HEAD_DIM], U8, align_bytes=64)
             nc.vector.quantize_mx(
                 out=v_codes[:].bitcast(FP8X4),
                 scales=v_scales[:],
-                in_=v_grouped[:].rearrange("p g d t -> p (g d t)"),
+                in_=v_grouped_of[h][:].rearrange("p g d t -> p (g d t)"),
             )
-            ready[h] = (kT, qT, v_codes, v_scales, near, far, far_step)
+            v_of[h] = (v_codes, v_scales)
 
-        def energies(n, h, b, g, r):
-            kT, qT, v_codes, v_scales, near, far, far_step = ready[h]
-            diagonal = g == b
-            live = r + 1 if diagonal else PACK
-            q_tile = b * TILES_PER_BLOCK + r
+        units = [(h, b, g) for h in range(HEADS) for b in range(N_BLOCKS) for g in range(b + 1)]
+
+        def live_tiles(n, r):
+            h, b, g = units[n]
+            return r + 1 if g == b else PACK
+
+        def far_scalar(n, r):
+            h, b, g = units[n]
+            near, far, far_step = decay_of[h]
+            s = (b - g - 1) * TILES_PER_BLOCK + r
+            return far_step[:, s : s + 1]
+
+        def fill(n, r):
+            h, b, g = units[n]
+            kq_cols = cols_of[h]
+            q_tile = N_TILES + b * TILES_PER_BLOCK + r
             s_bank = psum_s.tile([P, PACK, P], F32)
-            for t in range(live):
+            for t in range(live_tiles(n, r)):
                 k_tile = g * PACK + t
                 nc.tensor.matmul(
                     s_bank[:, t, :],
-                    lhsT=kT[:, k_tile * P : (k_tile + 1) * P],
-                    rhs=qT[:, q_tile * P : (q_tile + 1) * P],
+                    lhsT=kq_cols[:, k_tile * P : (k_tile + 1) * P],
+                    rhs=kq_cols[:, q_tile * P : (q_tile + 1) * P],
                     start=True,
                     stop=True,
                 )
-            s_view = s_bank[:, 0:live, :].rearrange("p t c -> p c t")
-            grouped = grouped_of[n]
-            if diagonal:
-                nc.vector.tensor_tensor(
-                    out=grouped[:, r, :, 0:live], in0=s_view, in1=near[:, :, PACK - live : PACK], op=ALU.mult
-                )
+            bank_of[(n, r)] = s_bank
+
+
+        def multiply(n, r):
+            h, b, g = units[n]
+            near, far, far_step = decay_of[h]
+            if r == 0:
+                if g == b:
+                    direct_of[n] = diag_tiles[(h * N_BLOCKS + b) % 2]
+                else:
+                    direct = work.tile([P, DIRECT, P, PACK], BF16, align_bytes=64)
+                    direct_of[n] = direct
+            live = live_tiles(n, r)
+            s_view = bank_of[(n, r)][:, 0:live, :].rearrange("p t c -> p c t")
+            energy = direct_of[n][:, r, :, 0:live]
+            if g == b:
+                nc.vector.tensor_tensor(out=energy, in0=s_view, in1=near[:, :, PACK - live : PACK], op=ALU.mult)
             else:
-                s = (b - g - 1) * TILES_PER_BLOCK + r
                 nc.vector.scalar_tensor_tensor(
-                    out=grouped[:, r, :, :],
-                    in0=s_view,
-                    scalar=far_step[:, s : s + 1],
-                    in1=far[:],
-                    op0=ALU.mult,
-                    op1=ALU.mult,
+                    out=energy, in0=s_view, scalar=far_scalar(n, r), in1=far[:], op0=ALU.mult, op1=ALU.mult
                 )
 
-        def quantise(n, h, b, g):
+        def lift(n):
+            h, b, g = units[n]
+            s_view = bank_of[(n, HELPED)][:].rearrange("p t c -> p c t")
+            lifted = work.tile([P, P, PACK], F32)
+            if g == b:
+                nc.scalar.copy(out=lifted[:], in_=s_view)
+            else:
+                nc.scalar.activation(out=lifted[:], in_=s_view, func=ACT.Copy, scale=far_scalar(n, HELPED))
+            lifted_of[n] = lifted
+
+        def help_multiply(n):
+            h, b, g = units[n]
+            near, far, far_step = decay_of[h]
+            helped = work.tile([P, P, PACK], BF16, align_bytes=64)
+            table = near if g == b else far
+            nc.gpsimd.tensor_tensor(out=helped[:], in0=lifted_of[n][:], in1=table[:], op=ALU.mult)
+            helped_of[n] = helped
+
+        def quantise(n):
+            h, b, g = units[n]
+            if g == 0:
+                e_codes = work.tile([P, N_BLOCKS, BLOCK], U32, align_bytes=64)
+                e_scales = work.tile([P, N_BLOCKS, BLOCK], U8, align_bytes=64)
+                codes_of[(h, b)] = (e_codes, e_scales)
             e_codes, e_scales = codes_of[(h, b)]
-            nc.vector.quantize_mx(
-                out=e_codes[:, g, :].bitcast(FP8X4),
-                scales=e_scales[:, g, :],
-                in_=grouped_of[n][:].rearrange("p r c t -> p (r c t)"),
-            )
+            direct = direct_of[n]
+            pieces = [
+                (0, direct[:, 0:2].rearrange("p r c t -> p (r c t)")),
+                (2, direct[:, 2:3].rearrange("p r c t -> p (r c t)")),
+                (HELPED, helped_of[n][:].rearrange("p c t -> p (c t)")),
+            ]
+            for r0, energy in pieces:
+                cols = slice(r0 * P, r0 * P + energy.shape[1] // PACK)
+                nc.vector.quantize_mx(
+                    out=e_codes[:, g, cols].bitcast(FP8X4), scales=e_scales[:, g, cols], in_=energy
+                )
 
         def second_matmul(h, b):
-            kT, qT, v_codes, v_scales, near, far, far_step = ready[h]
+            v_codes, v_scales = v_of[h]
             e_codes, e_scales = codes_of[(h, b)]
             o_bank = psum_o.tile([P, TILES_PER_BLOCK, HEAD_DIM], F32)
             for r in range(TILES_PER_BLOCK):
@@ -188,33 +253,39 @@ def tile_tnlattention_pa_kernel(tc, q, k, v, log_slope, out):
                 in_=o_rows[:],
             )
 
-        units = [(h, b, g) for h in range(HEADS) for b in range(N_BLOCKS) for g in range(b + 1)]
-
         load(0)
-        prepare(0)
         load(1)
-        for n, (h, b, g) in enumerate(units):
-            if g == 0:
-                e_codes = work.tile([P, N_BLOCKS, BLOCK], U32, align_bytes=64)
-                e_scales = work.tile([P, N_BLOCKS, BLOCK], U8, align_bytes=64)
-                codes_of[(h, b)] = (e_codes, e_scales)
-                if b == N_BLOCKS - 1 and h + 1 < HEADS:
-                    prepare(h + 1)
-                    if h + 2 < HEADS:
-                        load(h + 2)
-            if g == b:
-                grouped_of[n] = diag_tiles[(h * N_BLOCKS + b) % 2]
-            else:
-                grouped = work.tile([P, TILES_PER_BLOCK, P, PACK], BF16, align_bytes=64)
-                grouped_of[n] = grouped
-            for r in range(TILES_PER_BLOCK):
-                energies(n, h, b, g, r)
-                if r == 0 and n > 0:
-                    quantise(n - 1, *units[n - 1])
-            if n > 0:
-                h_done, b_done, g_done = units[n - 1]
-                if g_done == b_done:
-                    second_matmul(h_done, b_done)
-        last = len(units) - 1
-        quantise(last, *units[last])
-        second_matmul(HEADS - 1, N_BLOCKS - 1)
+        for u in range(FLIP_GROUPS):
+            prepare_step(0, u)
+        fill(0, HELPED)
+        lift(0)
+        for n in range(len(units) + 2):
+            filling = n < len(units)
+            multiplying = 1 <= n <= len(units)
+            quantising = n >= 2
+            if filling:
+                if n % UNITS_PER_HEAD == 0 and n // UNITS_PER_HEAD + 2 < HEADS:
+                    load(n // UNITS_PER_HEAD + 2)
+                fill(n, 0)
+                fill(n, 1)
+            if multiplying:
+                multiply(n - 1, 0)
+            if quantising:
+                quantise(n - 2)
+            if filling:
+                help_multiply(n)
+                fill(n, 2)
+            if multiplying:
+                multiply(n - 1, 1)
+                multiply(n - 1, 2)
+            if n + 1 < len(units):
+                fill(n + 1, HELPED)
+                lift(n + 1)
+            if filling and n % UNITS_PER_HEAD == 1:
+                quantise_v(n // UNITS_PER_HEAD)
+            if filling and n // UNITS_PER_HEAD + 1 < HEADS and n % UNITS_PER_HEAD < FLIP_GROUPS:
+                prepare_step(n // UNITS_PER_HEAD + 1, n % UNITS_PER_HEAD)
+            if quantising:
+                h, b, g = units[n - 2]
+                if g == b:
+                    second_matmul(h, b)

@@ -30,6 +30,7 @@ FLOPS = 2 * 2 * HEADS * HEAD_DIM * BLOCK * BLOCK * UNITS_PER_HEAD
 
 DIRECT = TILES_PER_BLOCK - 1
 HELPED = TILES_PER_BLOCK - 1
+RUN = 2
 
 
 def tile_tnlattention_pa_kernel(tc, q, k, v, log_slope, out):
@@ -124,15 +125,16 @@ def tile_tnlattention_pa_kernel(tc, q, k, v, log_slope, out):
                     out=cols_of[h][:, u * BLOCK : (u + 1) * BLOCK],
                     in_=flipped[:].rearrange("d j n -> d (j n)"),
                 )
-            if u == 0:
+
+        def regroup_v(h, g):
+            kq_rows, v_rows = rows_of[h]
+            if g == 0:
                 v_grouped = head.tile([P, N_BLOCKS, HEAD_DIM, PACK], BF16, align_bytes=64)
                 v_grouped_of[h] = v_grouped
-            if u >= FLIP_GROUPS - N_BLOCKS:
-                g = u - (FLIP_GROUPS - N_BLOCKS)
-                nc.scalar.copy(
-                    out=v_grouped_of[h][:, g],
-                    in_=v_rows[:, g * PACK : (g + 1) * PACK, :].rearrange("p t d -> p d t"),
-                )
+            nc.scalar.copy(
+                out=v_grouped_of[h][:, g],
+                in_=v_rows[:, g * PACK : (g + 1) * PACK, :].rearrange("p t d -> p d t"),
+            )
 
         def quantise_v(h):
             v_codes = head.tile([P, N_BLOCKS * HEAD_DIM], U32, align_bytes=64)
@@ -180,7 +182,7 @@ def tile_tnlattention_pa_kernel(tc, q, k, v, log_slope, out):
                 if g == b:
                     direct_of[n] = diag_tiles[(h * N_BLOCKS + b) % 2]
                 else:
-                    direct = work.tile([P, DIRECT, P, PACK], BF16, align_bytes=64)
+                    direct = work.tile([P, DIRECT, P, PACK], BF16, align_bytes=64, bufs=RUN + 1)
                     direct_of[n] = direct
             live = live_tiles(n, r)
             s_view = bank_of[(n, r)][:, 0:live, :].rearrange("p t c -> p c t")
@@ -195,7 +197,7 @@ def tile_tnlattention_pa_kernel(tc, q, k, v, log_slope, out):
         def lift(n):
             h, b, g = units[n]
             s_view = bank_of[(n, HELPED)][:].rearrange("p t c -> p c t")
-            lifted = work.tile([P, P, PACK], F32)
+            lifted = work.tile([P, P, PACK], F32, bufs=RUN + 2)
             if g == b:
                 nc.scalar.copy(out=lifted[:], in_=s_view)
             else:
@@ -205,29 +207,31 @@ def tile_tnlattention_pa_kernel(tc, q, k, v, log_slope, out):
         def help_multiply(n):
             h, b, g = units[n]
             near, far, far_step = decay_of[h]
-            helped = work.tile([P, P, PACK], BF16, align_bytes=64)
+            helped = work.tile([P, P, PACK], BF16, align_bytes=64, bufs=RUN)
             table = near if g == b else far
             nc.gpsimd.tensor_tensor(out=helped[:], in0=lifted_of[n][:], in1=table[:], op=ALU.mult)
             helped_of[n] = helped
 
-        def quantise(n):
+        def quantise(energy, n, r):
             h, b, g = units[n]
-            if g == 0:
-                e_codes = work.tile([P, N_BLOCKS, BLOCK], U32, align_bytes=64)
-                e_scales = work.tile([P, N_BLOCKS, BLOCK], U8, align_bytes=64)
-                codes_of[(h, b)] = (e_codes, e_scales)
             e_codes, e_scales = codes_of[(h, b)]
-            direct = direct_of[n]
-            pieces = [
-                (0, direct[:, 0:2].rearrange("p r c t -> p (r c t)")),
-                (2, direct[:, 2:3].rearrange("p r c t -> p (r c t)")),
-                (HELPED, helped_of[n][:].rearrange("p c t -> p (c t)")),
-            ]
-            for r0, energy in pieces:
-                cols = slice(r0 * P, r0 * P + energy.shape[1] // PACK)
-                nc.vector.quantize_mx(
-                    out=e_codes[:, g, cols].bitcast(FP8X4), scales=e_scales[:, g, cols], in_=energy
-                )
+            cols = slice(r * P, r * P + energy.shape[1] // PACK)
+            nc.vector.quantize_mx(out=e_codes[:, g, cols].bitcast(FP8X4), scales=e_scales[:, g, cols], in_=energy)
+
+        def quantise_run(first):
+            run = range(first, first + RUN)
+            for n in run:
+                h, b, g = units[n]
+                if n % UNITS_PER_HEAD == 0:
+                    quantise_v(h)
+                if g == 0:
+                    e_codes = work.tile([P, N_BLOCKS, BLOCK], U32, align_bytes=64)
+                    e_scales = work.tile([P, N_BLOCKS, BLOCK], U8, align_bytes=64)
+                    codes_of[(h, b)] = (e_codes, e_scales)
+                quantise(direct_of[n][:, 0:2].rearrange("p r c t -> p (r c t)"), n, 0)
+                quantise(direct_of[n][:, 2:3].rearrange("p r c t -> p (r c t)"), n, 2)
+            for n in run:
+                quantise(helped_of[n][:].rearrange("p c t -> p (c t)"), n, HELPED)
 
         def second_matmul(h, b):
             v_codes, v_scales = v_of[h]
@@ -257,12 +261,15 @@ def tile_tnlattention_pa_kernel(tc, q, k, v, log_slope, out):
         load(1)
         for u in range(FLIP_GROUPS):
             prepare_step(0, u)
-        fill(0, HELPED)
-        lift(0)
+        for early in range(RUN - 1):
+            fill(early, HELPED)
+            lift(early)
+        for g in range(N_BLOCKS):
+            regroup_v(0, g)
         for n in range(len(units) + 2):
             filling = n < len(units)
             multiplying = 1 <= n <= len(units)
-            quantising = n >= 2
+            turn = n % RUN == 1
             if filling:
                 if n % UNITS_PER_HEAD == 0 and n // UNITS_PER_HEAD + 2 < HEADS:
                     load(n // UNITS_PER_HEAD + 2)
@@ -270,22 +277,25 @@ def tile_tnlattention_pa_kernel(tc, q, k, v, log_slope, out):
                 fill(n, 1)
             if multiplying:
                 multiply(n - 1, 0)
-            if quantising:
-                quantise(n - 2)
+            if turn and n > RUN:
+                quantise_run(n - 1 - RUN)
+            if turn and filling:
+                for later in range(n - 1, n - 1 + RUN):
+                    help_multiply(later)
             if filling:
-                help_multiply(n)
                 fill(n, 2)
             if multiplying:
                 multiply(n - 1, 1)
                 multiply(n - 1, 2)
-            if n + 1 < len(units):
-                fill(n + 1, HELPED)
-                lift(n + 1)
-            if filling and n % UNITS_PER_HEAD == 1:
-                quantise_v(n // UNITS_PER_HEAD)
+            if n + RUN - 1 < len(units):
+                fill(n + RUN - 1, HELPED)
+                lift(n + RUN - 1)
             if filling and n // UNITS_PER_HEAD + 1 < HEADS and n % UNITS_PER_HEAD < FLIP_GROUPS:
                 prepare_step(n // UNITS_PER_HEAD + 1, n % UNITS_PER_HEAD)
-            if quantising:
-                h, b, g = units[n - 2]
-                if g == b:
-                    second_matmul(h, b)
+                if n % UNITS_PER_HEAD < N_BLOCKS:
+                    regroup_v(n // UNITS_PER_HEAD + 1, n % UNITS_PER_HEAD)
+            if turn and n > RUN:
+                for done in range(n - 1 - RUN, n - 1):
+                    h, b, g = units[done]
+                    if g == b:
+                        second_matmul(h, b)

@@ -31,6 +31,9 @@ FLOPS = 2 * 2 * HEADS * HEAD_DIM * BLOCK * BLOCK * UNITS_PER_HEAD
 DIRECT = TILES_PER_BLOCK - 1
 HELPED = TILES_PER_BLOCK - 1
 RUN = 2
+FAR = 0
+NEAR = 1
+TABLES_FROM = {(False, True): 0, (True, False): 1, (False, False): 2}
 
 
 def tile_tnlattention_pa_kernel(tc, q, k, v, log_slope, out):
@@ -102,20 +105,21 @@ def tile_tnlattention_pa_kernel(tc, q, k, v, log_slope, out):
             if u == 0:
                 kq_cols = head.tile([P, 2 * SEQ], BF16)
                 cols_of[h] = kq_cols
-                far = head.tile([P, P, PACK], F32)
-                nc.scalar.activation(
-                    out=far[:], in_=dist[:], func=ACT.Exp, bias=slope_tile[:, h : h + 1], scale=slope_h
-                )
+                tables = head.tile([P, 4, P, PACK], F32)
+                for place in range(4):
+                    if place != NEAR:
+                        nc.scalar.activation(
+                            out=tables[:, place], in_=dist[:], func=ACT.Exp, bias=slope_tile[:, h : h + 1], scale=slope_h
+                        )
                 near_raw = head.tile([P, P, PACK], F32)
                 nc.scalar.activation(out=near_raw[:], in_=dist_clamped[:], func=ACT.Exp, scale=slope_h)
+                raw_of[h] = near_raw
                 far_step = head.tile([P, FAR_STEPS], F32)
                 nc.scalar.activation(out=far_step[:], in_=step[:], func=ACT.Exp, scale=slope_h)
-                raw_of[h] = (near_raw, far, far_step)
-            if u == 1:
-                near_raw, far, far_step = raw_of[h]
-                near = head.tile([P, P, PACK], F32)
-                nc.vector.tensor_tensor(out=near[:], in0=near_raw[:], in1=causal[:], op=ALU.mult)
-                decay_of[h] = (near, far, far_step)
+                decay_of[h] = (tables, far_step)
+            if u == N_BLOCKS:
+                tables, far_step = decay_of[h]
+                nc.vector.tensor_tensor(out=tables[:, NEAR], in0=raw_of[h][:], in1=causal[:], op=ALU.mult)
             if u < FLIP_GROUPS:
                 tiles = kq_rows[:].rearrange("p a n d -> p (a n) d")
                 flipped = psum_t.tile([P, PACK, P], BF16)
@@ -154,7 +158,7 @@ def tile_tnlattention_pa_kernel(tc, q, k, v, log_slope, out):
 
         def far_scalar(n, r):
             h, b, g = units[n]
-            near, far, far_step = decay_of[h]
+            tables, far_step = decay_of[h]
             s = (b - g - 1) * TILES_PER_BLOCK + r
             return far_step[:, s : s + 1]
 
@@ -177,7 +181,7 @@ def tile_tnlattention_pa_kernel(tc, q, k, v, log_slope, out):
 
         def multiply(n, r):
             h, b, g = units[n]
-            near, far, far_step = decay_of[h]
+            tables, far_step = decay_of[h]
             if r == 0:
                 if g == b:
                     direct_of[n] = diag_tiles[(h * N_BLOCKS + b) % 2]
@@ -188,29 +192,35 @@ def tile_tnlattention_pa_kernel(tc, q, k, v, log_slope, out):
             s_view = bank_of[(n, r)][:, 0:live, :].rearrange("p t c -> p c t")
             energy = direct_of[n][:, r, :, 0:live]
             if g == b:
-                nc.vector.tensor_tensor(out=energy, in0=s_view, in1=near[:, :, PACK - live : PACK], op=ALU.mult)
+                nc.vector.tensor_tensor(out=energy, in0=s_view, in1=tables[:, NEAR, :, PACK - live : PACK], op=ALU.mult)
             else:
                 nc.vector.scalar_tensor_tensor(
-                    out=energy, in0=s_view, scalar=far_scalar(n, r), in1=far[:], op0=ALU.mult, op1=ALU.mult
+                    out=energy, in0=s_view, scalar=far_scalar(n, r), in1=tables[:, FAR], op0=ALU.mult, op1=ALU.mult
                 )
 
         def lift(n):
             h, b, g = units[n]
             s_view = bank_of[(n, HELPED)][:].rearrange("p t c -> p c t")
-            lifted = work.tile([P, P, PACK], F32, bufs=RUN + 2)
+            if n % RUN == 0:
+                lifted = work.tile([P, RUN, P, PACK], F32, bufs=3)
+                lifted_of[n // RUN] = lifted
             if g == b:
-                nc.scalar.copy(out=lifted[:], in_=s_view)
+                nc.scalar.copy(out=lifted_of[n // RUN][:, n % RUN], in_=s_view)
             else:
-                nc.scalar.activation(out=lifted[:], in_=s_view, func=ACT.Copy, scale=far_scalar(n, HELPED))
-            lifted_of[n] = lifted
+                nc.scalar.activation(
+                    out=lifted_of[n // RUN][:, n % RUN], in_=s_view, func=ACT.Copy, scale=far_scalar(n, HELPED)
+                )
 
-        def help_multiply(n):
-            h, b, g = units[n]
-            near, far, far_step = decay_of[h]
-            helped = work.tile([P, P, PACK], BF16, align_bytes=64, bufs=RUN)
-            table = near if g == b else far
-            nc.gpsimd.tensor_tensor(out=helped[:], in0=lifted_of[n][:], in1=table[:], op=ALU.mult)
-            helped_of[n] = helped
+        def help_multiply(first):
+            h, b, g = units[first]
+            h_next, b_next, g_next = units[first + 1]
+            tables, far_step = decay_of[h]
+            place = TABLES_FROM[(g == b, g_next == b_next)]
+            helped = work.tile([P, RUN, P, PACK], BF16, align_bytes=64, bufs=1)
+            nc.gpsimd.tensor_tensor(
+                out=helped[:], in0=lifted_of[first // RUN][:], in1=tables[:, place : place + RUN], op=ALU.mult
+            )
+            helped_of[first // RUN] = helped
 
         def quantise(energy, n, r):
             h, b, g = units[n]
@@ -231,7 +241,7 @@ def tile_tnlattention_pa_kernel(tc, q, k, v, log_slope, out):
                 quantise(direct_of[n][:, 0:2].rearrange("p r c t -> p (r c t)"), n, 0)
                 quantise(direct_of[n][:, 2:3].rearrange("p r c t -> p (r c t)"), n, 2)
             for n in run:
-                quantise(helped_of[n][:].rearrange("p c t -> p (c t)"), n, HELPED)
+                quantise(helped_of[n // RUN][:, n % RUN].rearrange("p c t -> p (c t)"), n, HELPED)
 
         def second_matmul(h, b):
             v_codes, v_scales = v_of[h]
@@ -280,8 +290,7 @@ def tile_tnlattention_pa_kernel(tc, q, k, v, log_slope, out):
             if turn and n > RUN:
                 quantise_run(n - 1 - RUN)
             if turn and filling:
-                for later in range(n - 1, n - 1 + RUN):
-                    help_multiply(later)
+                help_multiply(n - 1)
             if filling:
                 fill(n, 2)
             if multiplying:

@@ -28,12 +28,12 @@ FLIP_GROUPS = 2 * N_TILES // PACK
 FLOPS = 2 * 2 * HEADS * HEAD_DIM * BLOCK * BLOCK * UNITS_PER_HEAD
 
 
-DIRECT = TILES_PER_BLOCK - 1
-HELPED = TILES_PER_BLOCK - 1
+LAST = TILES_PER_BLOCK - 1
 RUN = 2
-FAR = 0
-NEAR = 1
-TABLES_FROM = {(False, True): 0, (True, False): 1, (False, False): 2}
+
+
+def helped_tile(diagonal):
+    return LAST - 1 if diagonal else LAST
 
 
 def tile_tnlattention_pa_kernel(tc, q, k, v, log_slope, out):
@@ -73,8 +73,8 @@ def tile_tnlattention_pa_kernel(tc, q, k, v, log_slope, out):
         slope_tile = const.tile([P, HEADS], F32)
         nc.vector.tensor_scalar_mul(out=slope_tile[:], in0=slope[:], scalar1=float(P))
 
-        diag_a = const.tile([P, DIRECT, P, PACK], BF16, align_bytes=64)
-        diag_b = const.tile([P, DIRECT, P, PACK], BF16, align_bytes=64)
+        diag_a = const.tile([P, LAST, P, PACK], BF16, align_bytes=64)
+        diag_b = const.tile([P, LAST, P, PACK], BF16, align_bytes=64)
         nc.vector.memset(diag_a[:], 0.0)
         nc.vector.memset(diag_b[:], 0.0)
         diag_tiles = [diag_a, diag_b]
@@ -87,8 +87,8 @@ def tile_tnlattention_pa_kernel(tc, q, k, v, log_slope, out):
         v_of = {}
         bank_of = {}
         lifted_of = {}
-        direct_of = {}
-        helped_of = {}
+        first_of = {}
+        last_of = {}
         codes_of = {}
 
         def load(h):
@@ -105,21 +105,20 @@ def tile_tnlattention_pa_kernel(tc, q, k, v, log_slope, out):
             if u == 0:
                 kq_cols = head.tile([P, 2 * SEQ], BF16)
                 cols_of[h] = kq_cols
-                tables = head.tile([P, 4, P, PACK], F32)
-                for place in range(4):
-                    if place != NEAR:
-                        nc.scalar.activation(
-                            out=tables[:, place], in_=dist[:], func=ACT.Exp, bias=slope_tile[:, h : h + 1], scale=slope_h
-                        )
+                far = head.tile([P, P, PACK], F32)
+                nc.scalar.activation(
+                    out=far[:], in_=dist[:], func=ACT.Exp, bias=slope_tile[:, h : h + 1], scale=slope_h
+                )
                 near_raw = head.tile([P, P, PACK], F32)
                 nc.scalar.activation(out=near_raw[:], in_=dist_clamped[:], func=ACT.Exp, scale=slope_h)
-                raw_of[h] = near_raw
                 far_step = head.tile([P, FAR_STEPS], F32)
                 nc.scalar.activation(out=far_step[:], in_=step[:], func=ACT.Exp, scale=slope_h)
-                decay_of[h] = (tables, far_step)
+                raw_of[h] = (near_raw, far, far_step)
             if u == N_BLOCKS:
-                tables, far_step = decay_of[h]
-                nc.vector.tensor_tensor(out=tables[:, NEAR], in0=raw_of[h][:], in1=causal[:], op=ALU.mult)
+                near_raw, far, far_step = raw_of[h]
+                near = head.tile([P, P, PACK], F32)
+                nc.vector.tensor_tensor(out=near[:], in0=near_raw[:], in1=causal[:], op=ALU.mult)
+                decay_of[h] = (near, far, far_step)
             if u < FLIP_GROUPS:
                 tiles = kq_rows[:].rearrange("p a n d -> p (a n) d")
                 flipped = psum_t.tile([P, PACK, P], BF16)
@@ -133,22 +132,25 @@ def tile_tnlattention_pa_kernel(tc, q, k, v, log_slope, out):
         def regroup_v(h, g):
             kq_rows, v_rows = rows_of[h]
             if g == 0:
-                v_grouped = head.tile([P, N_BLOCKS, HEAD_DIM, PACK], BF16, align_bytes=64)
+                v_grouped = head.tile([P, N_BLOCKS, HEAD_DIM, PACK], BF16, align_bytes=64, bufs=3)
                 v_grouped_of[h] = v_grouped
             nc.scalar.copy(
                 out=v_grouped_of[h][:, g],
                 in_=v_rows[:, g * PACK : (g + 1) * PACK, :].rearrange("p t d -> p d t"),
             )
 
-        def quantise_v(h):
-            v_codes = head.tile([P, N_BLOCKS * HEAD_DIM], U32, align_bytes=64)
-            v_scales = head.tile([P, N_BLOCKS * HEAD_DIM], U8, align_bytes=64)
+        def quantise_v(h, g):
+            if g == 0:
+                v_codes = head.tile([P, N_BLOCKS * HEAD_DIM], U32, align_bytes=64)
+                v_scales = head.tile([P, N_BLOCKS * HEAD_DIM], U8, align_bytes=64)
+                v_of[h] = (v_codes, v_scales)
+            v_codes, v_scales = v_of[h]
+            cols = slice(g * HEAD_DIM, (g + 1) * HEAD_DIM)
             nc.vector.quantize_mx(
-                out=v_codes[:].bitcast(FP8X4),
-                scales=v_scales[:],
-                in_=v_grouped_of[h][:].rearrange("p g d t -> p (g d t)"),
+                out=v_codes[:, cols].bitcast(FP8X4),
+                scales=v_scales[:, cols],
+                in_=v_grouped_of[h][:, g].rearrange("p d t -> p (d t)"),
             )
-            v_of[h] = (v_codes, v_scales)
 
         units = [(h, b, g) for h in range(HEADS) for b in range(N_BLOCKS) for g in range(b + 1)]
 
@@ -158,7 +160,7 @@ def tile_tnlattention_pa_kernel(tc, q, k, v, log_slope, out):
 
         def far_scalar(n, r):
             h, b, g = units[n]
-            tables, far_step = decay_of[h]
+            near, far, far_step = decay_of[h]
             s = (b - g - 1) * TILES_PER_BLOCK + r
             return far_step[:, s : s + 1]
 
@@ -179,48 +181,57 @@ def tile_tnlattention_pa_kernel(tc, q, k, v, log_slope, out):
             bank_of[(n, r)] = s_bank
 
 
+        def energy_of(n, r):
+            h, b, g = units[n]
+            if r == LAST:
+                if n not in last_of:
+                    last = work.tile([P, P, PACK], BF16, align_bytes=64, bufs=RUN)
+                    last_of[n] = last
+                return last_of[n][:]
+            if n not in first_of:
+                if g == b:
+                    first_of[n] = diag_tiles[(h * N_BLOCKS + b) % 2]
+                else:
+                    first = work.tile([P, LAST, P, PACK], BF16, align_bytes=64, bufs=RUN + 1)
+                    first_of[n] = first
+            return first_of[n][:, r, :, 0 : live_tiles(n, r)]
+
+        def table_of(n, r):
+            h, b, g = units[n]
+            near, far, far_step = decay_of[h]
+            return near[:, :, PACK - live_tiles(n, r) : PACK] if g == b else far[:]
+
         def multiply(n, r):
             h, b, g = units[n]
-            tables, far_step = decay_of[h]
-            if r == 0:
-                if g == b:
-                    direct_of[n] = diag_tiles[(h * N_BLOCKS + b) % 2]
-                else:
-                    direct = work.tile([P, DIRECT, P, PACK], BF16, align_bytes=64, bufs=RUN + 1)
-                    direct_of[n] = direct
-            live = live_tiles(n, r)
-            s_view = bank_of[(n, r)][:, 0:live, :].rearrange("p t c -> p c t")
-            energy = direct_of[n][:, r, :, 0:live]
+            s_view = bank_of[(n, r)][:, 0 : live_tiles(n, r), :].rearrange("p t c -> p c t")
             if g == b:
-                nc.vector.tensor_tensor(out=energy, in0=s_view, in1=tables[:, NEAR, :, PACK - live : PACK], op=ALU.mult)
+                nc.vector.tensor_tensor(out=energy_of(n, r), in0=s_view, in1=table_of(n, r), op=ALU.mult)
             else:
                 nc.vector.scalar_tensor_tensor(
-                    out=energy, in0=s_view, scalar=far_scalar(n, r), in1=tables[:, FAR], op0=ALU.mult, op1=ALU.mult
+                    out=energy_of(n, r),
+                    in0=s_view,
+                    scalar=far_scalar(n, r),
+                    in1=table_of(n, r),
+                    op0=ALU.mult,
+                    op1=ALU.mult,
                 )
 
         def lift(n):
             h, b, g = units[n]
-            s_view = bank_of[(n, HELPED)][:].rearrange("p t c -> p c t")
-            if n % RUN == 0:
-                lifted = work.tile([P, RUN, P, PACK], F32, bufs=3)
-                lifted_of[n // RUN] = lifted
+            r = helped_tile(g == b)
+            live = live_tiles(n, r)
+            s_view = bank_of[(n, r)][:, 0:live, :].rearrange("p t c -> p c t")
+            lifted = work.tile([P, P * PACK], F32, bufs=RUN + 2)
+            lifted_of[n] = lifted[:, 0 : P * live].rearrange("p (c t) -> p c t", t=live)
             if g == b:
-                nc.scalar.copy(out=lifted_of[n // RUN][:, n % RUN], in_=s_view)
+                nc.scalar.copy(out=lifted_of[n], in_=s_view)
             else:
-                nc.scalar.activation(
-                    out=lifted_of[n // RUN][:, n % RUN], in_=s_view, func=ACT.Copy, scale=far_scalar(n, HELPED)
-                )
+                nc.scalar.activation(out=lifted_of[n], in_=s_view, func=ACT.Copy, scale=far_scalar(n, r))
 
-        def help_multiply(first):
-            h, b, g = units[first]
-            h_next, b_next, g_next = units[first + 1]
-            tables, far_step = decay_of[h]
-            place = TABLES_FROM[(g == b, g_next == b_next)]
-            helped = work.tile([P, RUN, P, PACK], BF16, align_bytes=64, bufs=1)
-            nc.gpsimd.tensor_tensor(
-                out=helped[:], in0=lifted_of[first // RUN][:], in1=tables[:, place : place + RUN], op=ALU.mult
-            )
-            helped_of[first // RUN] = helped
+        def help_multiply(n):
+            h, b, g = units[n]
+            r = helped_tile(g == b)
+            nc.gpsimd.tensor_tensor(out=energy_of(n, r), in0=lifted_of[n], in1=table_of(n, r), op=ALU.mult)
 
         def quantise(energy, n, r):
             h, b, g = units[n]
@@ -232,16 +243,16 @@ def tile_tnlattention_pa_kernel(tc, q, k, v, log_slope, out):
             run = range(first, first + RUN)
             for n in run:
                 h, b, g = units[n]
-                if n % UNITS_PER_HEAD == 0:
-                    quantise_v(h)
+                if g == b:
+                    quantise_v(h, g)
                 if g == 0:
                     e_codes = work.tile([P, N_BLOCKS, BLOCK], U32, align_bytes=64)
                     e_scales = work.tile([P, N_BLOCKS, BLOCK], U8, align_bytes=64)
                     codes_of[(h, b)] = (e_codes, e_scales)
-                quantise(direct_of[n][:, 0:2].rearrange("p r c t -> p (r c t)"), n, 0)
-                quantise(direct_of[n][:, 2:3].rearrange("p r c t -> p (r c t)"), n, 2)
+                quantise(first_of[n][:, 0:2].rearrange("p r c t -> p (r c t)"), n, 0)
+                quantise(first_of[n][:, 2:3].rearrange("p r c t -> p (r c t)"), n, 2)
             for n in run:
-                quantise(helped_of[n // RUN][:, n % RUN].rearrange("p c t -> p (c t)"), n, HELPED)
+                quantise(last_of[n][:].rearrange("p c t -> p (c t)"), n, LAST)
 
         def second_matmul(h, b):
             v_codes, v_scales = v_of[h]
@@ -267,42 +278,50 @@ def tile_tnlattention_pa_kernel(tc, q, k, v, log_slope, out):
                 in_=o_rows[:],
             )
 
+        def helped(n):
+            h, b, g = units[n]
+            return helped_tile(g == b)
+
+        def direct(n):
+            return [r for r in range(TILES_PER_BLOCK) if r != helped(n)]
+
         load(0)
         load(1)
         for u in range(FLIP_GROUPS):
             prepare_step(0, u)
         for early in range(RUN - 1):
-            fill(early, HELPED)
+            fill(early, helped(early))
             lift(early)
-        for g in range(N_BLOCKS):
-            regroup_v(0, g)
         for n in range(len(units) + 2):
             filling = n < len(units)
             multiplying = 1 <= n <= len(units)
             turn = n % RUN == 1
             if filling:
-                if n % UNITS_PER_HEAD == 0 and n // UNITS_PER_HEAD + 2 < HEADS:
+                if n % UNITS_PER_HEAD == N_BLOCKS and n // UNITS_PER_HEAD + 2 < HEADS:
                     load(n // UNITS_PER_HEAD + 2)
-                fill(n, 0)
-                fill(n, 1)
+                fill(n, direct(n)[0])
+                fill(n, direct(n)[1])
             if multiplying:
-                multiply(n - 1, 0)
+                multiply(n - 1, direct(n - 1)[0])
             if turn and n > RUN:
                 quantise_run(n - 1 - RUN)
             if turn and filling:
-                help_multiply(n - 1)
+                for later in sorted(range(n - 1, n - 1 + RUN), key=helped, reverse=True):
+                    help_multiply(later)
             if filling:
-                fill(n, 2)
+                fill(n, direct(n)[2])
             if multiplying:
-                multiply(n - 1, 1)
-                multiply(n - 1, 2)
+                multiply(n - 1, direct(n - 1)[1])
+                multiply(n - 1, direct(n - 1)[2])
             if n + RUN - 1 < len(units):
-                fill(n + RUN - 1, HELPED)
+                fill(n + RUN - 1, helped(n + RUN - 1))
                 lift(n + RUN - 1)
+            if n < N_BLOCKS:
+                regroup_v(0, n)
             if filling and n // UNITS_PER_HEAD + 1 < HEADS and n % UNITS_PER_HEAD < FLIP_GROUPS:
                 prepare_step(n // UNITS_PER_HEAD + 1, n % UNITS_PER_HEAD)
-                if n % UNITS_PER_HEAD < N_BLOCKS:
-                    regroup_v(n // UNITS_PER_HEAD + 1, n % UNITS_PER_HEAD)
+                if n % UNITS_PER_HEAD >= N_BLOCKS:
+                    regroup_v(n // UNITS_PER_HEAD + 1, n % UNITS_PER_HEAD - N_BLOCKS)
             if turn and n > RUN:
                 for done in range(n - 1 - RUN, n - 1):
                     h, b, g = units[done]

from contextlib import ExitStack

import concourse.mybir as mybir
from concourse.masks import make_identity

F32 = mybir.dt.float32
BF16 = mybir.dt.bfloat16
I32 = mybir.dt.int32
U32 = mybir.dt.uint32
U8 = mybir.dt.uint8
FP8X4 = mybir.dt.float8_e4m3fn_x4
ALU = mybir.AluOpType
ACT = mybir.ActivationFunctionType

P = 128
PACK = 4
HEADS = 8
SEQ = 2048
HEAD_DIM = 128
BLOCK = 512
N_TILES = SEQ // P
N_BLOCKS = SEQ // BLOCK
TILES_PER_BLOCK = BLOCK // P
UNITS_PER_HEAD = N_BLOCKS * (N_BLOCKS + 1) // 2
FAR_STEPS = N_TILES - PACK
FLIP_GROUPS = 2 * N_TILES // PACK

FLOPS = 2 * 2 * HEADS * HEAD_DIM * BLOCK * BLOCK * UNITS_PER_HEAD


LAST = TILES_PER_BLOCK - 1
RUN = 2


def helped_tile(diagonal):
    return LAST - 1 if diagonal else LAST


def tile_tnlattention_pa_kernel(tc, q, k, v, log_slope, out):
    nc = tc.nc
    with ExitStack() as ctx:
        const = ctx.enter_context(tc.tile_pool(name="const", bufs=1))
        rows = ctx.enter_context(tc.tile_pool(name="rows", bufs=2))
        head = ctx.enter_context(tc.tile_pool(name="head", bufs=2))
        work = ctx.enter_context(tc.tile_pool(name="work", bufs=2))
        psum_s = ctx.enter_context(tc.psum_pool(name="psum_s", bufs=5))
        psum_o = ctx.enter_context(tc.psum_pool(name="psum_o", bufs=1))
        psum_t = ctx.enter_context(tc.psum_pool(name="psum_t", bufs=2))
        ctx.enter_context(tc.manual_schedule())

        slope_bf = const.tile([P, HEADS], BF16)
        nc.sync.dma_start(out=slope_bf[:], in_=log_slope.partition_broadcast(P))

        ident = const.tile([P, P], BF16)
        make_identity(nc, ident[:])

        dist_int = const.tile([P, P, PACK], I32)
        nc.gpsimd.iota(dist_int[:], pattern=[[1, P], [-P, PACK]], base=(PACK - 1) * P, channel_multiplier=-1)
        step_int = const.tile([P, FAR_STEPS], I32)
        nc.gpsimd.iota(step_int[:], pattern=[[P, FAR_STEPS]], base=0, channel_multiplier=0)

        dist = const.tile([P, P, PACK], F32)
        nc.vector.tensor_copy(out=dist[:], in_=dist_int[:])
        dist_clamped = const.tile([P, P, PACK], F32)
        nc.vector.tensor_scalar_max(out=dist_clamped[:], in0=dist[:], scalar1=0.0)
        causal = const.tile([P, P, PACK], F32)
        nc.vector.tensor_single_scalar(out=causal[:], in_=dist[:], scalar=0.0, op=ALU.is_ge)
        step = const.tile([P, FAR_STEPS], F32)
        nc.vector.tensor_copy(out=step[:], in_=step_int[:])

        slope = const.tile([P, HEADS], F32)
        nc.vector.tensor_copy(out=slope[:], in_=slope_bf[:])
        slope_tile = const.tile([P, HEADS], F32)
        nc.vector.tensor_scalar_mul(out=slope_tile[:], in0=slope[:], scalar1=float(P))

        diag_a = const.tile([P, LAST, P, PACK], BF16, align_bytes=64)
        diag_b = const.tile([P, LAST, P, PACK], BF16, align_bytes=64)
        nc.vector.memset(diag_a[:], 0.0)
        nc.vector.memset(diag_b[:], 0.0)
        diag_tiles = [diag_a, diag_b]

        rows_of = {}
        cols_of = {}
        raw_of = {}
        decay_of = {}
        v_grouped_of = {}
        v_of = {}
        bank_of = {}
        lifted_of = {}
        first_of = {}
        last_of = {}
        codes_of = {}

        def load(h):
            kq_rows = rows.tile([P, 2, N_TILES, HEAD_DIM], BF16)
            v_rows = rows.tile([P, N_TILES, HEAD_DIM], BF16)
            nc.sync.dma_start(out=kq_rows[:, 0], in_=k[0, h].rearrange("(n p) d -> p n d", p=P))
            nc.sync.dma_start(out=kq_rows[:, 1], in_=q[0, h].rearrange("(n p) d -> p n d", p=P))
            nc.sync.dma_start(out=v_rows[:], in_=v[0, h].rearrange("(n p) d -> p n d", p=P))
            rows_of[h] = (kq_rows, v_rows)

        def prepare_step(h, u):
            kq_rows, v_rows = rows_of[h]
            slope_h = slope[:, h : h + 1]
            if u == 0:
                kq_cols = head.tile([P, 2 * SEQ], BF16)
                cols_of[h] = kq_cols
                far = head.tile([P, P, PACK], F32)
                nc.scalar.activation(
                    out=far[:], in_=dist[:], func=ACT.Exp, bias=slope_tile[:, h : h + 1], scale=slope_h
                )
                near_raw = head.tile([P, P, PACK], F32)
                nc.scalar.activation(out=near_raw[:], in_=dist_clamped[:], func=ACT.Exp, scale=slope_h)
                far_step = head.tile([P, FAR_STEPS], F32)
                nc.scalar.activation(out=far_step[:], in_=step[:], func=ACT.Exp, scale=slope_h)
                raw_of[h] = (near_raw, far, far_step)
            if u == N_BLOCKS:
                near_raw, far, far_step = raw_of[h]
                near = head.tile([P, P, PACK], F32)
                nc.vector.tensor_tensor(out=near[:], in0=near_raw[:], in1=causal[:], op=ALU.mult)
                decay_of[h] = (near, far, far_step)
            if u < FLIP_GROUPS:
                tiles = kq_rows[:].rearrange("p a n d -> p (a n) d")
                flipped = psum_t.tile([P, PACK, P], BF16)
                for j in range(PACK):
                    nc.tensor.transpose(flipped[:, j, :], tiles[:, u * PACK + j, :], ident[:])
                nc.scalar.copy(
                    out=cols_of[h][:, u * BLOCK : (u + 1) * BLOCK],
                    in_=flipped[:].rearrange("d j n -> d (j n)"),
                )

        def regroup_v(h, g):
            kq_rows, v_rows = rows_of[h]
            if g == 0:
                v_grouped = head.tile([P, N_BLOCKS, HEAD_DIM, PACK], BF16, align_bytes=64, bufs=3)
                v_grouped_of[h] = v_grouped
            nc.scalar.copy(
                out=v_grouped_of[h][:, g],
                in_=v_rows[:, g * PACK : (g + 1) * PACK, :].rearrange("p t d -> p d t"),
            )

        def quantise_v(h, g):
            if g == 0:
                v_codes = head.tile([P, N_BLOCKS * HEAD_DIM], U32, align_bytes=64)
                v_scales = head.tile([P, N_BLOCKS * HEAD_DIM], U8, align_bytes=64)
                v_of[h] = (v_codes, v_scales)
            v_codes, v_scales = v_of[h]
            cols = slice(g * HEAD_DIM, (g + 1) * HEAD_DIM)
            nc.vector.quantize_mx(
                out=v_codes[:, cols].bitcast(FP8X4),
                scales=v_scales[:, cols],
                in_=v_grouped_of[h][:, g].rearrange("p d t -> p (d t)"),
            )

        units = [(h, b, g) for h in range(HEADS) for b in range(N_BLOCKS) for g in range(b + 1)]

        def live_tiles(n, r):
            h, b, g = units[n]
            return r + 1 if g == b else PACK

        def far_scalar(n, r):
            h, b, g = units[n]
            near, far, far_step = decay_of[h]
            s = (b - g - 1) * TILES_PER_BLOCK + r
            return far_step[:, s : s + 1]

        def fill(n, r):
            h, b, g = units[n]
            kq_cols = cols_of[h]
            q_tile = N_TILES + b * TILES_PER_BLOCK + r
            s_bank = psum_s.tile([P, PACK, P], F32)
            for t in range(live_tiles(n, r)):
                k_tile = g * PACK + t
                nc.tensor.matmul(
                    s_bank[:, t, :],
                    lhsT=kq_cols[:, k_tile * P : (k_tile + 1) * P],
                    rhs=kq_cols[:, q_tile * P : (q_tile + 1) * P],
                    start=True,
                    stop=True,
                )
            bank_of[(n, r)] = s_bank


        def energy_of(n, r):
            h, b, g = units[n]
            if r == LAST:
                if n not in last_of:
                    last = work.tile([P, P, PACK], BF16, align_bytes=64, bufs=RUN)
                    last_of[n] = last
                return last_of[n][:]
            if n not in first_of:
                if g == b:
                    first_of[n] = diag_tiles[(h * N_BLOCKS + b) % 2]
                else:
                    first = work.tile([P, LAST, P, PACK], BF16, align_bytes=64, bufs=RUN + 1)
                    first_of[n] = first
            return first_of[n][:, r, :, 0 : live_tiles(n, r)]

        def table_of(n, r):
            h, b, g = units[n]
            near, far, far_step = decay_of[h]
            return near[:, :, PACK - live_tiles(n, r) : PACK] if g == b else far[:]

        def multiply(n, r):
            h, b, g = units[n]
            s_view = bank_of[(n, r)][:, 0 : live_tiles(n, r), :].rearrange("p t c -> p c t")
            if g == b:
                nc.vector.tensor_tensor(out=energy_of(n, r), in0=s_view, in1=table_of(n, r), op=ALU.mult)
            else:
                nc.vector.scalar_tensor_tensor(
                    out=energy_of(n, r),
                    in0=s_view,
                    scalar=far_scalar(n, r),
                    in1=table_of(n, r),
                    op0=ALU.mult,
                    op1=ALU.mult,
                )

        def lift(n):
            h, b, g = units[n]
            r = helped_tile(g == b)
            live = live_tiles(n, r)
            s_view = bank_of[(n, r)][:, 0:live, :].rearrange("p t c -> p c t")
            lifted = work.tile([P, P * PACK], F32, bufs=RUN + 2)
            lifted_of[n] = lifted[:, 0 : P * live].rearrange("p (c t) -> p c t", t=live)
            if g == b:
                nc.scalar.copy(out=lifted_of[n], in_=s_view)
            else:
                nc.scalar.activation(out=lifted_of[n], in_=s_view, func=ACT.Copy, scale=far_scalar(n, r))

        def help_multiply(n):
            h, b, g = units[n]
            r = helped_tile(g == b)
            nc.gpsimd.tensor_tensor(out=energy_of(n, r), in0=lifted_of[n], in1=table_of(n, r), op=ALU.mult)

        def quantise(energy, n, r):
            h, b, g = units[n]
            e_codes, e_scales = codes_of[(h, b)]
            cols = slice(r * P, r * P + energy.shape[1] // PACK)
            nc.vector.quantize_mx(out=e_codes[:, g, cols].bitcast(FP8X4), scales=e_scales[:, g, cols], in_=energy)

        def quantise_run(first):
            run = range(first, first + RUN)
            for n in run:
                h, b, g = units[n]
                if g == b:
                    quantise_v(h, g)
                if g == 0:
                    e_codes = work.tile([P, N_BLOCKS, BLOCK], U32, align_bytes=64)
                    e_scales = work.tile([P, N_BLOCKS, BLOCK], U8, align_bytes=64)
                    codes_of[(h, b)] = (e_codes, e_scales)
                quantise(first_of[n][:, 0:2].rearrange("p r c t -> p (r c t)"), n, 0)
                quantise(first_of[n][:, 2:3].rearrange("p r c t -> p (r c t)"), n, 2)
            for n in run:
                quantise(last_of[n][:].rearrange("p c t -> p (c t)"), n, LAST)

        def second_matmul(h, b):
            v_codes, v_scales = v_of[h]
            e_codes, e_scales = codes_of[(h, b)]
            o_bank = psum_o.tile([P, TILES_PER_BLOCK, HEAD_DIM], F32)
            for r in range(TILES_PER_BLOCK):
                q_cols = slice(r * P, (r + 1) * P)
                for g in range(b + 1):
                    v_cols = slice(g * HEAD_DIM, (g + 1) * HEAD_DIM)
                    nc.tensor.matmul_mx(
                        out=o_bank[:, r, :],
                        lhsT=e_codes[:, g, q_cols].bitcast(FP8X4),
                        lhsT_scale=e_scales[:, g, q_cols],
                        rhs=v_codes[:, v_cols].bitcast(FP8X4),
                        rhs_scale=v_scales[:, v_cols],
                        start=(g == 0),
                        stop=(g == b),
                    )
            o_rows = work.tile([P, TILES_PER_BLOCK, HEAD_DIM], F32)
            nc.scalar.copy(out=o_rows[:], in_=o_bank[:])
            nc.sync.dma_start(
                out=out[0, h, b * BLOCK : (b + 1) * BLOCK, :].rearrange("(r p) d -> p r d", p=P),
                in_=o_rows[:],
            )

        def helped(n):
            h, b, g = units[n]
            return helped_tile(g == b)

        def direct(n):
            return [r for r in range(TILES_PER_BLOCK) if r != helped(n)]

        load(0)
        load(1)
        for u in range(FLIP_GROUPS):
            prepare_step(0, u)
        for early in range(RUN - 1):
            fill(early, helped(early))
            lift(early)
        for n in range(len(units) + 2):
            filling = n < len(units)
            multiplying = 1 <= n <= len(units)
            turn = n % RUN == 1
            if filling:
                if n % UNITS_PER_HEAD == N_BLOCKS and n // UNITS_PER_HEAD + 2 < HEADS:
                    load(n // UNITS_PER_HEAD + 2)
                fill(n, direct(n)[0])
                fill(n, direct(n)[1])
            if multiplying:
                multiply(n - 1, direct(n - 1)[0])
            if turn and n > RUN:
                quantise_run(n - 1 - RUN)
            if turn and filling:
                for later in sorted(range(n - 1, n - 1 + RUN), key=helped, reverse=True):
                    help_multiply(later)
            if filling:
                fill(n, direct(n)[2])
            if multiplying:
                multiply(n - 1, direct(n - 1)[1])
                multiply(n - 1, direct(n - 1)[2])
            if n + RUN - 1 < len(units):
                fill(n + RUN - 1, helped(n + RUN - 1))
                lift(n + RUN - 1)
            if n < N_BLOCKS:
                regroup_v(0, n)
            if filling and n // UNITS_PER_HEAD + 1 < HEADS and n % UNITS_PER_HEAD < FLIP_GROUPS:
                prepare_step(n // UNITS_PER_HEAD + 1, n % UNITS_PER_HEAD)
                if n % UNITS_PER_HEAD >= N_BLOCKS:
                    regroup_v(n // UNITS_PER_HEAD + 1, n % UNITS_PER_HEAD - N_BLOCKS)
            if turn and n > RUN:
                for done in range(n - 1 - RUN, n - 1):
                    h, b, g = units[done]
                    if g == b:
                        second_matmul(h, b)
